import numpy as np
import ml_dtypes


def mxq(x, axis, fmt="e4m3"):
    dtype, down = {"e4m3": (ml_dtypes.float8_e4m3fn, 7), "e5m2": (ml_dtypes.float8_e5m2, 14)}[fmt]
    v = np.moveaxis(np.asarray(x, np.float32).astype(ml_dtypes.bfloat16).astype(np.float64), axis, -1)
    blocks = v.reshape(v.shape[:-1] + (-1, 32))
    amax = np.abs(blocks).max(-1, keepdims=True)
    byte = np.maximum(np.where(amax > 0, np.frexp(amax)[1] - 1 + 127, 0) - down, 1)
    scale = np.exp2(byte - 127.0)
    codes = (blocks / scale).astype(np.float32).astype(dtype).astype(np.float64)
    return np.moveaxis((codes * scale).reshape(v.shape), -1, axis)


WIDE = False


def mx_kscale(k):
    if not WIDE:
        return np.ones(k)
    levels = np.array([10, -10, 5, -5, 0])
    if k % 512:
        return np.exp2(np.random.permutation(np.resize(levels, k // 32))).repeat(32)
    a = np.empty((k // 512, 16))
    for p in range(k // 512):
        a[p, :8] = np.random.permutation(np.resize(levels, 8))
        for g in range(8):
            far = levels[np.abs(levels - a[p, g]) >= 10]
            a[p, g + 8] = far[np.random.randint(len(far))]
    return np.exp2(a.ravel()).repeat(32)


BF16 = ml_dtypes.bfloat16


def bf(x):
    return np.asarray(x, np.float32).astype(BF16)


def f64(x):
    return np.asarray(x).astype(np.float64)


B, D, H, F, C, R = 8192, 512, 1024, 1024, 128, 32
P_FACTOR = 3.0
RHO = 0.75
P_LABEL = 0.1


def unit_rows(x):
    return x / np.sqrt((x ** 2).sum(-1, keepdims=True))


def draw0():
    s = mx_kscale(F)
    u = np.exp2(np.round(np.log2(mx_kscale(D)) / P_FACTOR))
    basis = np.random.standard_normal((R, F))
    off = np.random.standard_normal(F) * 0.1
    f = np.random.standard_normal((B, R)) @ basis * np.sqrt(RHO / R) + np.sqrt(1.0 - RHO) * np.random.standard_normal((B, F)) + off
    e = np.random.standard_normal((D, R)) @ basis * np.sqrt(RHO / R) + np.sqrt(1.0 - RHO) * np.random.standard_normal((D, F)) + off
    return {"f_n": bf(unit_rows(f) * s),
            "ex_n": bf(unit_rows(e) / s * u[:, None]),
            "ex_classes": bf((np.random.uniform(size=(D, C)) < P_LABEL) / (u * u * u)[:, None]),
            "class_reps": bf(np.eye(C) + np.random.standard_normal((C, C)) / np.sqrt(C))}


def core(f_n, ex_n, ex_classes, class_reps):
    s = mxq(f64(f_n), 1, "e4m3") @ mxq(f64(ex_n), 1, "e4m3").T
    a = np.sign(s) * np.abs(s) ** P_FACTOR
    ex_class_reps = f64(ex_classes) @ f64(class_reps)
    echo = mxq(a, 1, "e4m3") @ mxq(ex_class_reps, 0, "e4m3")
    d2 = np.stack([((echo - r) ** 2).sum(-1) for r in f64(class_reps)], axis=1)
    return -np.sqrt(d2)


def e4m3fn_bytes(y):
    return np.clip(np.asarray(y, np.float64), -448.0, 448.0).astype(np.float32).astype(ml_dtypes.float8_e4m3fn).view(np.uint8)


def e4m3fn_values(b):
    return np.asarray(b, np.uint8).view(ml_dtypes.float8_e4m3fn).astype(np.float64)


def setup_inputs():
    d = draw0()
    x0 = np.asarray(d['f_n']).astype(np.float64)
    s = (np.max(np.abs(x0), axis=(0,), keepdims=True) / 448.0).astype(np.float32)
    out = {}
    for k, v in d.items():
        if k == 'f_n':
            out['f_n_bytes'] = e4m3fn_bytes(x0 / s.astype(np.float64))
            out['f_n_scale'] = s
        else:
            out[k] = v
    return out


def reference(f_n_bytes, f_n_scale, ex_n, ex_classes, class_reps):
    return core(e4m3fn_values(f_n_bytes) * f_n_scale.astype(np.float64), ex_n, ex_classes, class_reps)

@@ -1,0 +1,320 @@
+from contextlib import ExitStack
+
+import concourse.mybir as mybir
+from concourse.masks import make_identity
+
+B, D, H, C = 8192, 512, 1024, 128
+P = 128
+
+FLOPS = 2 * B * D * H + 2 * D * C * C + 2 * B * D * C + 3 * B * C * C
+
+F32 = mybir.dt.float32
+BF16 = mybir.dt.bfloat16
+U32 = mybir.dt.uint32
+U8 = mybir.dt.uint8
+FP8 = mybir.dt.float8_e4m3fn
+FP8X4 = mybir.dt.float8_e4m3fn_x4
+ACT = mybir.ActivationFunctionType
+MULT = mybir.AluOpType.mult
+SUB = mybir.AluOpType.subtract
+
+BLK = 512
+NBLK = B // BLK
+PAIRS = 2 * NBLK
+
+
+def tile_minerva_detex_pb_t_kernel(tc, f_bytes, f_scale, ex_n, ex_classes, class_reps, out):
+    nc = tc.nc
+    x_view = f_bytes.rearrange("(s p h j) k -> s h p (j k)", p=P, h=2, j=2)
+    out_view = out.rearrange("(s p j) k -> s p j k", p=P, j=4)
+
+    with ExitStack() as ctx:
+        keep = ctx.enter_context(tc.tile_pool(name="keep", bufs=1))
+        xin = ctx.enter_context(tc.tile_pool(name="xin", bufs=16))
+        work = ctx.enter_context(tc.tile_pool(name="work", bufs=3))
+        sqp = ctx.enter_context(tc.tile_pool(name="sqp", bufs=4))
+        epi = ctx.enter_context(tc.tile_pool(name="epi", bufs=2))
+        ps_x = ctx.enter_context(tc.psum_pool(name="ps_x", bufs=2))
+        ps_s = ctx.enter_context(tc.psum_pool(name="ps_s", bufs=4))
+        ps_e = ctx.enter_context(tc.psum_pool(name="ps_e", bufs=2))
+
+        x_tiles, xs_tiles, xt_tiles, xg_tiles, xq_tiles = {}, {}, {}, {}, {}
+        s_tiles, sq_tiles, a_tiles, aq_tiles, e_tiles = {}, {}, {}, {}, {}
+
+        tiny = keep.tile([P, 1], F32)
+        warm = keep.tile([P, 1], F32)
+        id_f = keep.tile([P, P], F32)
+        id_b = keep.tile([P, P], BF16)
+        ones_f = keep.tile([P, P], F32)
+        ones_b = keep.tile([P, P], BF16)
+        scale = keep.tile([P, 2 * H], F32)
+        ex_raw = keep.tile([P, 4, H], BF16, align_bytes=64)
+        ex_grp = keep.tile([P, 4 * H], BF16, align_bytes=64)
+        ex_codes = keep.tile([P, H], U32, align_bytes=64)
+        ex_scales = keep.tile([P, H], U8, align_bytes=64)
+        cls_raw = keep.tile([P, 4, C], BF16)
+        cls_t = keep.tile([P, 4, P], BF16)
+        reps = keep.tile([P, C], BF16)
+        ec_grp = keep.tile([P, 4 * C], BF16, align_bytes=64)
+        ec_codes = keep.tile([P, C], U32, align_bytes=64)
+        ec_scales = keep.tile([P, C], U8, align_bytes=64)
+        reps_m2 = keep.tile([P, C], F32)
+        reps_sq = keep.tile([P, C], F32)
+        n_hi = keep.tile([P, C], BF16)
+        n_mid = keep.tile([P, C], BF16)
+        n_lo = keep.tile([P, C], BF16)
+        n_all = keep.tile([P, C], F32)
+        n_d1 = keep.tile([P, C], F32)
+        n_d2 = keep.tile([P, C], F32)
+        norms = keep.tile([P, C], BF16)
+
+        def load(pair):
+            xb = xin.tile([P, 2 * H], U8)
+            nc.sync.dma_start(out=xb[:], in_=x_view[pair // 2, pair % 2])
+            x_tiles[pair] = xb
+
+        def widen(pair):
+            xs = work.tile([P, 2 * H], BF16, align_bytes=64)
+            xb = x_tiles[pair]
+            step = H // 2 if pair == 0 else 2 * H
+            for c in range(0, 2 * H, step):
+                nc.vector.tensor_tensor(
+                    out=xs[:, c : c + step],
+                    in0=xb[:, c : c + step].bitcast(FP8),
+                    in1=scale[:, c % H : c % H + step],
+                    op=MULT,
+                )
+            xs_tiles[pair] = xs
+
+        def turn(words, bank):
+            for g in range(2):
+                for u in range(2):
+                    nc.tensor.transpose(bank[:, 2 * g + u, :], words[:, 256 * g + u : 256 * (g + 1) : 2], id_f[:])
+
+        def leave(grouped_words, bank):
+            nc.scalar.copy(
+                out=grouped_words.rearrange("p (g r u) -> p g r u", g=2, u=2),
+                in_=bank[:].rearrange("p (g u) r -> p g r u", g=2),
+            )
+
+        def transposes(pair):
+            for j in range(2):
+                xt = ps_x.tile([P, 4, P], F32)
+                turn(xs_tiles[pair][:, j * H : (j + 1) * H].bitcast(F32), xt)
+                xt_tiles[pair, j] = xt
+
+        def regroup(pair):
+            xg = work.tile([P, 2 * H], BF16, align_bytes=64)
+            for j in range(2):
+                leave(xg[:, j * H : (j + 1) * H].bitcast(F32), xt_tiles[pair, j])
+            xg_tiles[pair] = xg
+
+        def quantize_x(pair):
+            xc = work.tile([P, H // 2], U32, align_bytes=64)
+            xp = work.tile([P, H // 2], U8, align_bytes=64)
+            nc.vector.quantize_mx(out=xc[:].bitcast(FP8X4), scales=xp[:], in_=xg_tiles[pair][:])
+            xq_tiles[pair] = (xc, xp)
+
+        def similarity(pair):
+            xc, xp = xq_tiles[pair]
+            for j in range(2):
+                s_ps = ps_s.tile([P, 4, P], F32)
+                for t in range(4):
+                    for g in range(2):
+                        w = slice((2 * t + g) * P, (2 * t + g + 1) * P)
+                        m = slice((2 * j + g) * P, (2 * j + g + 1) * P)
+                        nc.tensor.matmul_mx(
+                            out=s_ps[:, t, :],
+                            lhsT=ex_codes[:, w].bitcast(FP8X4),
+                            lhsT_scale=ex_scales[:, w],
+                            rhs=xc[:, m].bitcast(FP8X4),
+                            rhs_scale=xp[:, m],
+                            start=(g == 0),
+                            stop=(g == 1),
+                        )
+                s_tiles[pair, j] = s_ps
+
+        def squares(pair):
+            for j in range(2):
+                sq = sqp.tile([P, P, 4], F32)
+                nc.scalar.activation(out=sq[:], in_=s_tiles[pair, j][:].rearrange("p t r -> p r t"), func=ACT.Square)
+                sq_tiles[pair, j] = sq
+
+        def cubes(pair):
+            blk = pair // 2
+            if pair % 2 == 0:
+                a_grp = epi.tile([P, BLK, 4], BF16, align_bytes=64)
+                a_tiles[blk] = a_grp
+            for j in range(2):
+                c0 = (2 * (pair % 2) + j) * P
+                nc.vector.tensor_tensor(
+                    out=a_tiles[blk][:, c0 : c0 + P, :],
+                    in0=s_tiles[pair, j][:].rearrange("p t r -> p r t"),
+                    in1=sq_tiles[pair, j][:],
+                    op=MULT,
+                )
+
+        def quantize_a(chunk):
+            blk, lo, n = chunk
+            ac = epi.tile([P, BLK], U32, align_bytes=64)
+            ap = epi.tile([P, BLK], U8, align_bytes=64)
+            cols = slice(lo * P, (lo + n) * P)
+            nc.vector.quantize_mx(
+                out=ac[:, cols].bitcast(FP8X4),
+                scales=ap[:, cols],
+                in_=a_tiles[blk][:, cols, :].rearrange("p r t -> p (r t)"),
+            )
+            aq_tiles[chunk] = (ac, ap)
+
+        def echoes(chunk):
+            blk, lo, n = chunk
+            ac, ap = aq_tiles[chunk]
+            span = slice(lo * P, (lo + n) * P)
+            et_ps = ps_e.tile([P, BLK], F32, tag="ep")
+            nc.tensor.matmul_mx(
+                out=et_ps[:, span],
+                lhsT=ec_codes[:].bitcast(FP8X4),
+                lhsT_scale=ec_scales[:],
+                rhs=ac[:, span].bitcast(FP8X4),
+                rhs_scale=ap[:, span],
+                start=True,
+                stop=True,
+            )
+            e_ps = ps_e.tile([P, 4, C], F32, tag="ep")
+            for j in range(lo, lo + n):
+                cols = slice(j * P, (j + 1) * P)
+                nc.tensor.matmul_mx(
+                    out=e_ps[:, j, :],
+                    lhsT=ac[:, cols].bitcast(FP8X4),
+                    lhsT_scale=ap[:, cols],
+                    rhs=ec_codes[:].bitcast(FP8X4),
+                    rhs_scale=ec_scales[:],
+                    start=True,
+                    stop=True,
+                )
+            et = epi.tile([P, BLK], F32)
+            nc.scalar.copy(out=et[:, span], in_=et_ps[:, span])
+            e2 = epi.tile([P, 4], F32)
+            for j in range(lo, lo + n):
+                junk = epi.tile([P, C], F32)
+                nc.scalar.activation(out=junk[:], in_=e_ps[:, j, :], func=ACT.Square, accum_out=e2[:, j : j + 1])
+            e_tiles[chunk] = (et, e2)
+
+        def products(chunk):
+            blk, lo, n = chunk
+            et, e2 = e_tiles[chunk]
+            d_ps = ps_e.tile([P, 4, C], F32, tag="ep")
+            for j in range(lo, lo + n):
+                nc.tensor.matmul(d_ps[:, j, :], et[:, j * P : (j + 1) * P], reps_m2[:], start=True, stop=False)
+                nc.tensor.matmul(d_ps[:, j, :], ones_b[:], norms[:], start=False, stop=True)
+            d2 = epi.tile([P, 4, C], F32)
+            for j in range(lo, lo + n):
+                nc.scalar.activation(out=d2[:, j, :], in_=d_ps[:, j, :], func=ACT.Relu, bias=e2[:, j : j + 1])
+            e_tiles[chunk] = d2
+
+        def roots(chunk):
+            blk, lo, n = chunk
+            root = epi.tile([P, 4, C], F32)
+            nc.scalar.activation(
+                out=root[:, lo : lo + n, :], in_=e_tiles[chunk][:, lo : lo + n, :], func=ACT.Sqrt, bias=tiny[:]
+            )
+            e_tiles[chunk] = root
+
+        def finish(chunk):
+            blk, lo, n = chunk
+            root = e_tiles[chunk]
+            res = epi.tile([P, 4, C], F32)
+            if blk == NBLK - 1:
+                nc.vector.tensor_scalar(
+                    out=res[:, lo : lo + n, :], in0=root[:, lo : lo + n, :], scalar1=-1.0, scalar2=None, op0=MULT
+                )
+            else:
+                nc.scalar.mul(res[:, lo : lo + n, :], root[:, lo : lo + n, :], -1.0)
+            nc.sync.dma_start(out=out_view[blk, :, lo : lo + n, :], in_=res[:, lo : lo + n, :])
+
+        def setup_exemplars():
+            for t in range(4):
+                xt = ps_x.tile([P, 4, P], F32)
+                turn(ex_raw[:, t, :].bitcast(F32), xt)
+                leave(ex_grp[:, t * H : (t + 1) * H].bitcast(F32), xt)
+            for c in range(2):
+                w = slice(c * H // 2, (c + 1) * H // 2)
+                nc.vector.quantize_mx(
+                    out=ex_codes[:, w].bitcast(FP8X4), scales=ex_scales[:, w], in_=ex_grp[:, 2 * c * H : 2 * (c + 1) * H]
+                )
+
+        def setup_classes():
+            ct_ps = ps_e.tile([P, 4, P], BF16, tag="ep")
+            for t in range(4):
+                nc.tensor.transpose(ct_ps[:, t, :], cls_raw[:, t, :], id_b[:])
+            nc.scalar.copy(out=cls_t[:], in_=ct_ps[:])
+            rt_ps = ps_e.tile([P, C], BF16, tag="ep")
+            nc.tensor.transpose(rt_ps[:], reps[:], id_b[:])
+            nc.scalar.activation(out=reps_m2[:], in_=rt_ps[:], func=ACT.Copy, scale=-2.0)
+            nc.scalar.activation(out=reps_sq[:], in_=rt_ps[:], func=ACT.Square)
+            ec_ps = ps_e.tile([P, 4, C], F32, tag="ep")
+            for t in range(4):
+                nc.tensor.matmul(ec_ps[:, t, :], cls_t[:, t, :], reps[:], start=True, stop=True)
+            nc.scalar.copy(out=ec_grp[:].rearrange("p (c t) -> p c t", t=4), in_=ec_ps[:].rearrange("p t c -> p c t"))
+            n_ps = ps_e.tile([P, C], F32, tag="ep")
+            nc.tensor.matmul(n_ps[:], ones_f[:], reps_sq[:], start=True, stop=True)
+            nc.scalar.copy(out=n_all[:], in_=n_ps[:])
+            nc.vector.quantize_mx(out=ec_codes[:].bitcast(FP8X4), scales=ec_scales[:], in_=ec_grp[:])
+            nc.gpsimd.tensor_copy(out=n_hi[:], in_=n_all[:])
+            nc.gpsimd.tensor_tensor(out=n_d1[:], in0=n_all[:], in1=n_hi[:], op=SUB)
+            nc.gpsimd.tensor_copy(out=n_mid[:], in_=n_d1[:])
+            nc.gpsimd.tensor_tensor(out=n_d2[:], in0=n_d1[:], in1=n_mid[:], op=SUB)
+            nc.gpsimd.tensor_copy(out=n_lo[:], in_=n_d2[:])
+            nc.gpsimd.tensor_scalar(out=norms[0:32, :], in0=n_hi[0:32, :], scalar1=1.0 / 32, scalar2=None, op0=MULT)
+            nc.gpsimd.tensor_scalar(out=norms[32:64, :], in0=n_mid[32:64, :], scalar1=1.0 / 32, scalar2=None, op0=MULT)
+            nc.gpsimd.tensor_scalar(out=norms[64:96, :], in0=n_lo[64:96, :], scalar1=1.0 / 32, scalar2=None, op0=MULT)
+
+        with tc.manual_schedule():
+            nc.vector.memset(tiny[:], 2.0**-100)
+            nc.scalar.activation(out=warm[:], in_=tiny[:], func=ACT.Sqrt)
+            scale_row = f_scale.rearrange("o k -> (o k)")
+            for c in range(0, H, H // 2):
+                nc.scalar.dma_start(out=scale[:, c : c + H // 2], in_=scale_row[c : c + H // 2].partition_broadcast(P))
+            load(0)
+            ex_view = ex_n.rearrange("(m t) k -> m t k", t=4)
+            for t in range(4):
+                nc.sync.dma_start(out=ex_raw[:, t, :], in_=ex_view[:, t, :])
+            nc.sync.dma_start(out=cls_raw[:], in_=ex_classes.rearrange("(m t) c -> m t c", t=4))
+            nc.sync.dma_start(out=reps[:], in_=class_reps)
+            make_identity(nc, id_f[:])
+            make_identity(nc, id_b[:])
+            nc.gpsimd.memset(ones_b[:], 1.0)
+            nc.gpsimd.memset(ones_f[:], 1.0)
+            nc.gpsimd.memset(norms[:], 0.0)
+            for pair in range(1, 8):
+                load(pair)
+            chunks = [(blk, 0, 4) for blk in range(NBLK - 1)] + [(NBLK - 1, 0, 2), (NBLK - 1, 2, 2)]
+            last_pair = {2 * blk + (lo + n) // 2 - 1: (blk, lo, n) for blk, lo, n in chunks}
+            widen(0)
+            nc.scalar.copy(out=scale[:, H : 2 * H], in_=scale[:, 0:H])
+            setup_exemplars()
+            for i in range(PAIRS + 5):
+                if 8 + i < PAIRS:
+                    load(8 + i)
+                if i < PAIRS:
+                    if i > 0:
+                        widen(i)
+                    transposes(i)
+                    regroup(i)
+                if i == 1:
+                    setup_classes()
+                if i - 4 in last_pair:
+                    products(last_pair[i - 4])
+                if i - 3 in last_pair:
+                    quantize_a(last_pair[i - 3])
+                    echoes(last_pair[i - 3])
+                if 1 <= i <= PAIRS:
+                    quantize_x(i - 1)
+                    similarity(i - 1)
+                    squares(i - 1)
+                if 2 <= i <= PAIRS + 1:
+                    cubes(i - 2)
+                if i - 4 in last_pair:
+                    roots(last_pair[i - 4])
+                if i - 5 in last_pair:
+                    finish(last_pair[i - 5])

@@ -18,28 +18,27 @@ ACT = mybir.ActivationFunctionType
 MULT = mybir.AluOpType.mult
 SUB = mybir.AluOpType.subtract
 
-BLK = 512
-NBLK = B // BLK
-PAIRS = 2 * NBLK
+UNITS = B // P
+GROUP = 4
+LEAD = 10
 
 
 def tile_minerva_detex_pb_t_kernel(tc, f_bytes, f_scale, ex_n, ex_classes, class_reps, out):
     nc = tc.nc
     x_view = f_bytes.rearrange("(s p h j) k -> s h p (j k)", p=P, h=2, j=2)
-    out_view = out.rearrange("(s p j) k -> s p j k", p=P, j=4)
+    out_view = out.rearrange("(s p j) k -> s p j k", p=P, j=GROUP)
 
     with ExitStack() as ctx:
         keep = ctx.enter_context(tc.tile_pool(name="keep", bufs=1))
         xin = ctx.enter_context(tc.tile_pool(name="xin", bufs=16))
-        work = ctx.enter_context(tc.tile_pool(name="work", bufs=3))
-        sqp = ctx.enter_context(tc.tile_pool(name="sqp", bufs=4))
-        epi = ctx.enter_context(tc.tile_pool(name="epi", bufs=2))
-        ps_x = ctx.enter_context(tc.psum_pool(name="ps_x", bufs=2))
-        ps_s = ctx.enter_context(tc.psum_pool(name="ps_s", bufs=4))
-        ps_e = ctx.enter_context(tc.psum_pool(name="ps_e", bufs=2))
+        work = ctx.enter_context(tc.tile_pool(name="work", bufs=4))
+        ps_x = ctx.enter_context(tc.psum_pool(name="ps_x", bufs=3))
+        ps_s = ctx.enter_context(tc.psum_pool(name="ps_s", bufs=2))
+        ps_e = ctx.enter_context(tc.psum_pool(name="ps_e", bufs=3))
 
         x_tiles, xs_tiles, xt_tiles, xg_tiles, xq_tiles = {}, {}, {}, {}, {}
-        s_tiles, sq_tiles, a_tiles, aq_tiles, e_tiles = {}, {}, {}, {}, {}
+        s_tiles, sq_tiles, a_tiles, aq_tiles = {}, {}, {}, {}
+        ep_tiles, e_tiles, d2_tiles, root_tiles, res_tiles = {}, {}, {}, {}, {}
 
         tiny = keep.tile([P, 1], F32)
         warm = keep.tile([P, 1], F32)
@@ -47,7 +46,8 @@ def tile_minerva_detex_pb_t_kernel(tc, f_bytes, f_scale, ex_n, ex_classes, class
         id_b = keep.tile([P, P], BF16)
         ones_f = keep.tile([P, P], F32)
         ones_b = keep.tile([P, P], BF16)
-        scale = keep.tile([P, 2 * H], F32)
+        scale_row = keep.tile([P, H], F32)
+        scale = keep.tile([P, H], F32)
         ex_raw = keep.tile([P, 4, H], BF16, align_bytes=64)
         ex_grp = keep.tile([P, 4 * H], BF16, align_bytes=64)
         ex_codes = keep.tile([P, H], U32, align_bytes=64)
@@ -60,183 +60,177 @@ def tile_minerva_detex_pb_t_kernel(tc, f_bytes, f_scale, ex_n, ex_classes, class
         ec_scales = keep.tile([P, C], U8, align_bytes=64)
         reps_m2 = keep.tile([P, C], F32)
         reps_sq = keep.tile([P, C], F32)
+        n_all = keep.tile([P, C], F32)
         n_hi = keep.tile([P, C], BF16)
         n_mid = keep.tile([P, C], BF16)
         n_lo = keep.tile([P, C], BF16)
-        n_all = keep.tile([P, C], F32)
         n_d1 = keep.tile([P, C], F32)
         n_d2 = keep.tile([P, C], F32)
         norms = keep.tile([P, C], BF16)
 
         def load(pair):
             xb = xin.tile([P, 2 * H], U8)
-            nc.sync.dma_start(out=xb[:], in_=x_view[pair // 2, pair % 2])
+            src = x_view[pair // 2, pair % 2]
+            step = H if pair == 0 else 2 * H
+            for c in range(0, 2 * H, step):
+                nc.sync.dma_start(out=xb[:, c : c + step], in_=src[:, c : c + step])
             x_tiles[pair] = xb
 
-        def widen(pair):
-            xs = work.tile([P, 2 * H], BF16, align_bytes=64)
-            xb = x_tiles[pair]
-            step = H // 2 if pair == 0 else 2 * H
-            for c in range(0, 2 * H, step):
+        def widen(u):
+            xs = work.tile([P, H], BF16, align_bytes=64)
+            c0 = (u % 2) * H
+            step = H // 2 if u == 0 else H
+            for c in range(0, H, step):
                 nc.vector.tensor_tensor(
                     out=xs[:, c : c + step],
-                    in0=xb[:, c : c + step].bitcast(FP8),
-                    in1=scale[:, c % H : c % H + step],
+                    in0=x_tiles[u // 2][:, c0 + c : c0 + c + step].bitcast(FP8),
+                    in1=scale[:, c : c + step],
                     op=MULT,
                 )
-            xs_tiles[pair] = xs
+            xs_tiles[u] = xs
 
         def turn(words, bank):
             for g in range(2):
-                for u in range(2):
-                    nc.tensor.transpose(bank[:, 2 * g + u, :], words[:, 256 * g + u : 256 * (g + 1) : 2], id_f[:])
+                for h in range(2):
+                    nc.tensor.transpose(bank[:, 2 * g + h, :], words[:, 256 * g + h : 256 * (g + 1) : 2], id_f[:])
 
         def leave(grouped_words, bank):
             nc.scalar.copy(
-                out=grouped_words.rearrange("p (g r u) -> p g r u", g=2, u=2),
-                in_=bank[:].rearrange("p (g u) r -> p g r u", g=2),
+                out=grouped_words.rearrange("p (g r h) -> p g r h", g=2, h=2),
+                in_=bank[:].rearrange("p (g h) r -> p g r h", g=2),
             )
 
-        def transposes(pair):
-            for j in range(2):
-                xt = ps_x.tile([P, 4, P], F32)
-                turn(xs_tiles[pair][:, j * H : (j + 1) * H].bitcast(F32), xt)
-                xt_tiles[pair, j] = xt
+        def transposes(u):
+            xt = ps_x.tile([P, 4, P], F32, tag="xt")
+            turn(xs_tiles[u][:].bitcast(F32), xt)
+            xt_tiles[u] = xt
 
-        def regroup(pair):
-            xg = work.tile([P, 2 * H], BF16, align_bytes=64)
-            for j in range(2):
-                leave(xg[:, j * H : (j + 1) * H].bitcast(F32), xt_tiles[pair, j])
-            xg_tiles[pair] = xg
+        def regroup(u):
+            xg = work.tile([P, H], BF16, align_bytes=64)
+            leave(xg[:].bitcast(F32), xt_tiles[u])
+            xg_tiles[u] = xg
 
-        def quantize_x(pair):
-            xc = work.tile([P, H // 2], U32, align_bytes=64)
-            xp = work.tile([P, H // 2], U8, align_bytes=64)
-            nc.vector.quantize_mx(out=xc[:].bitcast(FP8X4), scales=xp[:], in_=xg_tiles[pair][:])
-            xq_tiles[pair] = (xc, xp)
+        def quantize_x(u):
+            xc = work.tile([P, 2 * P], U32, align_bytes=64)
+            xp = work.tile([P, 2 * P], U8, align_bytes=64)
+            nc.vector.quantize_mx(out=xc[:].bitcast(FP8X4), scales=xp[:], in_=xg_tiles[u][:])
+            xq_tiles[u] = (xc, xp)
 
-        def similarity(pair):
-            xc, xp = xq_tiles[pair]
-            for j in range(2):
-                s_ps = ps_s.tile([P, 4, P], F32)
-                for t in range(4):
-                    for g in range(2):
-                        w = slice((2 * t + g) * P, (2 * t + g + 1) * P)
-                        m = slice((2 * j + g) * P, (2 * j + g + 1) * P)
-                        nc.tensor.matmul_mx(
-                            out=s_ps[:, t, :],
-                            lhsT=ex_codes[:, w].bitcast(FP8X4),
-                            lhsT_scale=ex_scales[:, w],
-                            rhs=xc[:, m].bitcast(FP8X4),
-                            rhs_scale=xp[:, m],
-                            start=(g == 0),
-                            stop=(g == 1),
-                        )
-                s_tiles[pair, j] = s_ps
+        def similarity(u):
+            xc, xp = xq_tiles[u]
+            s_ps = ps_s.tile([P, 4, P], F32, tag="s")
+            for t in range(4):
+                for g in range(2):
+                    w = slice((2 * t + g) * P, (2 * t + g + 1) * P)
+                    m = slice(g * P, (g + 1) * P)
+                    nc.tensor.matmul_mx(
+                        out=s_ps[:, t, :],
+                        lhsT=ex_codes[:, w].bitcast(FP8X4),
+                        lhsT_scale=ex_scales[:, w],
+                        rhs=xc[:, m].bitcast(FP8X4),
+                        rhs_scale=xp[:, m],
+                        start=(g == 0),
+                        stop=(g == 1),
+                    )
+            s_tiles[u] = s_ps
 
-        def squares(pair):
-            for j in range(2):
-                sq = sqp.tile([P, P, 4], F32)
-                nc.scalar.activation(out=sq[:], in_=s_tiles[pair, j][:].rearrange("p t r -> p r t"), func=ACT.Square)
-                sq_tiles[pair, j] = sq
+        def squares(u):
+            sq = work.tile([P, P, 4], F32)
+            nc.scalar.activation(out=sq[:], in_=s_tiles[u][:].rearrange("p t r -> p r t"), func=ACT.Square)
+            sq_tiles[u] = sq
 
-        def cubes(pair):
-            blk = pair // 2
-            if pair % 2 == 0:
-                a_grp = epi.tile([P, BLK, 4], BF16, align_bytes=64)
-                a_tiles[blk] = a_grp
-            for j in range(2):
-                c0 = (2 * (pair % 2) + j) * P
-                nc.vector.tensor_tensor(
-                    out=a_tiles[blk][:, c0 : c0 + P, :],
-                    in0=s_tiles[pair, j][:].rearrange("p t r -> p r t"),
-                    in1=sq_tiles[pair, j][:],
-                    op=MULT,
-                )
+        def cubes(u):
+            a_grp = work.tile([P, P, 4], BF16, align_bytes=64)
+            nc.vector.tensor_tensor(
+                out=a_grp[:], in0=s_tiles[u][:].rearrange("p t r -> p r t"), in1=sq_tiles[u][:], op=MULT
+            )
+            a_tiles[u] = a_grp
 
-        def quantize_a(chunk):
-            blk, lo, n = chunk
-            ac = epi.tile([P, BLK], U32, align_bytes=64)
-            ap = epi.tile([P, BLK], U8, align_bytes=64)
-            cols = slice(lo * P, (lo + n) * P)
+        def quantize_a(u):
+            ac = work.tile([P, P], U32, align_bytes=64)
+            ap = work.tile([P, P], U8, align_bytes=64)
             nc.vector.quantize_mx(
-                out=ac[:, cols].bitcast(FP8X4),
-                scales=ap[:, cols],
-                in_=a_tiles[blk][:, cols, :].rearrange("p r t -> p (r t)"),
+                out=ac[:].bitcast(FP8X4), scales=ap[:], in_=a_tiles[u][:].rearrange("p r t -> p (r t)")
             )
-            aq_tiles[chunk] = (ac, ap)
+            aq_tiles[u] = (ac, ap)
 
-        def echoes(chunk):
-            blk, lo, n = chunk
-            ac, ap = aq_tiles[chunk]
-            span = slice(lo * P, (lo + n) * P)
-            et_ps = ps_e.tile([P, BLK], F32, tag="ep")
+        def echoes(u):
+            ac, ap = aq_tiles[u]
+            ep = ps_e.tile([P, 4, P], F32, tag="ep")
             nc.tensor.matmul_mx(
-                out=et_ps[:, span],
+                out=ep[:, 0, :],
                 lhsT=ec_codes[:].bitcast(FP8X4),
                 lhsT_scale=ec_scales[:],
-                rhs=ac[:, span].bitcast(FP8X4),
-                rhs_scale=ap[:, span],
+                rhs=ac[:].bitcast(FP8X4),
+                rhs_scale=ap[:],
                 start=True,
                 stop=True,
             )
-            e_ps = ps_e.tile([P, 4, C], F32, tag="ep")
-            for j in range(lo, lo + n):
-                cols = slice(j * P, (j + 1) * P)
-                nc.tensor.matmul_mx(
-                    out=e_ps[:, j, :],
-                    lhsT=ac[:, cols].bitcast(FP8X4),
-                    lhsT_scale=ap[:, cols],
-                    rhs=ec_codes[:].bitcast(FP8X4),
-                    rhs_scale=ec_scales[:],
-                    start=True,
-                    stop=True,
-                )
-            et = epi.tile([P, BLK], F32)
-            nc.scalar.copy(out=et[:, span], in_=et_ps[:, span])
-            e2 = epi.tile([P, 4], F32)
-            for j in range(lo, lo + n):
-                junk = epi.tile([P, C], F32)
-                nc.scalar.activation(out=junk[:], in_=e_ps[:, j, :], func=ACT.Square, accum_out=e2[:, j : j + 1])
-            e_tiles[chunk] = (et, e2)
-
-        def products(chunk):
-            blk, lo, n = chunk
-            et, e2 = e_tiles[chunk]
-            d_ps = ps_e.tile([P, 4, C], F32, tag="ep")
-            for j in range(lo, lo + n):
-                nc.tensor.matmul(d_ps[:, j, :], et[:, j * P : (j + 1) * P], reps_m2[:], start=True, stop=False)
-                nc.tensor.matmul(d_ps[:, j, :], ones_b[:], norms[:], start=False, stop=True)
-            d2 = epi.tile([P, 4, C], F32)
-            for j in range(lo, lo + n):
-                nc.scalar.activation(out=d2[:, j, :], in_=d_ps[:, j, :], func=ACT.Relu, bias=e2[:, j : j + 1])
-            e_tiles[chunk] = d2
-
-        def roots(chunk):
-            blk, lo, n = chunk
-            root = epi.tile([P, 4, C], F32)
-            nc.scalar.activation(
-                out=root[:, lo : lo + n, :], in_=e_tiles[chunk][:, lo : lo + n, :], func=ACT.Sqrt, bias=tiny[:]
+            nc.tensor.matmul_mx(
+                out=ep[:, 1, :],
+                lhsT=ac[:].bitcast(FP8X4),
+                lhsT_scale=ap[:],
+                rhs=ec_codes[:].bitcast(FP8X4),
+                rhs_scale=ec_scales[:],
+                start=True,
+                stop=True,
             )
-            e_tiles[chunk] = root
+            ep_tiles[u] = ep
 
-        def finish(chunk):
-            blk, lo, n = chunk
-            root = e_tiles[chunk]
-            res = epi.tile([P, 4, C], F32)
-            if blk == NBLK - 1:
-                nc.vector.tensor_scalar(
-                    out=res[:, lo : lo + n, :], in0=root[:, lo : lo + n, :], scalar1=-1.0, scalar2=None, op0=MULT
-                )
-            else:
-                nc.scalar.mul(res[:, lo : lo + n, :], root[:, lo : lo + n, :], -1.0)
-            nc.sync.dma_start(out=out_view[blk, :, lo : lo + n, :], in_=res[:, lo : lo + n, :])
+        def echo_out(u):
+            ep = ep_tiles[u]
+            et = work.tile([P, P], F32)
+            nc.scalar.copy(out=et[:], in_=ep[:, 0, :])
+            junk = work.tile([P, C], F32)
+            e2 = work.tile([P, 1], F32)
+            nc.scalar.activation(out=junk[:], in_=ep[:, 1, :], func=ACT.Square, accum_out=e2[:])
+            e_tiles[u] = (et, e2)
 
-        def setup_exemplars():
+        def products(u):
+            et, e2 = e_tiles[u]
+            d_ps = ep_tiles[u][:, 2, :]
+            nc.tensor.matmul(d_ps, ones_b[:], norms[:], start=True, stop=False)
+            nc.tensor.matmul(d_ps, et[:], reps_m2[:], start=False, stop=True)
+
+        def distances(u):
+            et, e2 = e_tiles[u]
+            d2 = work.tile([P, C], F32)
+            nc.scalar.activation(out=d2[:], in_=ep_tiles[u][:, 2, :], func=ACT.Relu, bias=e2[:])
+            d2_tiles[u] = d2
+
+        def roots(u):
+            root = work.tile([P, C], F32)
+            nc.scalar.activation(out=root[:], in_=d2_tiles[u][:], func=ACT.Sqrt, bias=tiny[:])
+            root_tiles[u] = root
+
+        def finish(u):
+            blk, j = u // GROUP, u % GROUP
+            if j == 0:
+                res = work.tile([P, GROUP, C], F32)
+                res_tiles[blk] = res
+            nc.scalar.mul(res_tiles[blk][:, j, :], root_tiles[u][:], -1.0)
+            width = 1 if blk == UNITS // GROUP - 1 else GROUP
+            if (j + 1) % width == 0:
+                js = slice(j + 1 - width, j + 1)
+                nc.sync.dma_start(out=out_view[blk, :, js, :], in_=res_tiles[blk][:, js, :])
+
+        def spread_scale():
+            for c in range(2):
+                half = slice(c * H // 2, (c + 1) * H // 2)
+                s_ps = ps_s.tile([P, H // 2], F32, tag="s")
+                nc.tensor.matmul(s_ps[:], ones_f[:], scale_row[:, half], start=True, stop=True)
+                if c == 0:
+                    nc.vector.tensor_copy(out=scale[:, half], in_=s_ps[:])
+                else:
+                    nc.scalar.copy(out=scale[:, half], in_=s_ps[:])
+
+        def turn_exemplars():
             for t in range(4):
-                xt = ps_x.tile([P, 4, P], F32)
+                xt = ps_x.tile([P, 4, P], F32, tag="xt")
                 turn(ex_raw[:, t, :].bitcast(F32), xt)
                 leave(ex_grp[:, t * H : (t + 1) * H].bitcast(F32), xt)
+
+        def quantize_exemplars():
             for c in range(2):
                 w = slice(c * H // 2, (c + 1) * H // 2)
                 nc.vector.quantize_mx(
@@ -247,19 +241,20 @@ def tile_minerva_detex_pb_t_kernel(tc, f_bytes, f_scale, ex_n, ex_classes, class
             ct_ps = ps_e.tile([P, 4, P], BF16, tag="ep")
             for t in range(4):
                 nc.tensor.transpose(ct_ps[:, t, :], cls_raw[:, t, :], id_b[:])
-            nc.scalar.copy(out=cls_t[:], in_=ct_ps[:])
             rt_ps = ps_e.tile([P, C], BF16, tag="ep")
             nc.tensor.transpose(rt_ps[:], reps[:], id_b[:])
+            nc.scalar.copy(out=cls_t[:], in_=ct_ps[:])
             nc.scalar.activation(out=reps_m2[:], in_=rt_ps[:], func=ACT.Copy, scale=-2.0)
             nc.scalar.activation(out=reps_sq[:], in_=rt_ps[:], func=ACT.Square)
+
+        def multiply_classes():
             ec_ps = ps_e.tile([P, 4, C], F32, tag="ep")
             for t in range(4):
                 nc.tensor.matmul(ec_ps[:, t, :], cls_t[:, t, :], reps[:], start=True, stop=True)
-            nc.scalar.copy(out=ec_grp[:].rearrange("p (c t) -> p c t", t=4), in_=ec_ps[:].rearrange("p t c -> p c t"))
             n_ps = ps_e.tile([P, C], F32, tag="ep")
             nc.tensor.matmul(n_ps[:], ones_f[:], reps_sq[:], start=True, stop=True)
+            nc.scalar.copy(out=ec_grp[:].rearrange("p (c t) -> p c t", t=4), in_=ec_ps[:].rearrange("p t c -> p c t"))
             nc.scalar.copy(out=n_all[:], in_=n_ps[:])
-            nc.vector.quantize_mx(out=ec_codes[:].bitcast(FP8X4), scales=ec_scales[:], in_=ec_grp[:])
             nc.gpsimd.tensor_copy(out=n_hi[:], in_=n_all[:])
             nc.gpsimd.tensor_tensor(out=n_d1[:], in0=n_all[:], in1=n_hi[:], op=SUB)
             nc.gpsimd.tensor_copy(out=n_mid[:], in_=n_d1[:])
@@ -269,52 +264,52 @@ def tile_minerva_detex_pb_t_kernel(tc, f_bytes, f_scale, ex_n, ex_classes, class
             nc.gpsimd.tensor_scalar(out=norms[32:64, :], in0=n_mid[32:64, :], scalar1=1.0 / 32, scalar2=None, op0=MULT)
             nc.gpsimd.tensor_scalar(out=norms[64:96, :], in0=n_lo[64:96, :], scalar1=1.0 / 32, scalar2=None, op0=MULT)
 
+        def quantize_classes():
+            nc.vector.quantize_mx(out=ec_codes[:].bitcast(FP8X4), scales=ec_scales[:], in_=ec_grp[:])
+
+        steps = [
+            (finish, 11),
+            (widen, 0),
+            (quantize_x, 2),
+            (transposes, 1),
+            (squares, 4),
+            (regroup, 1),
+            (quantize_a, 5),
+            (echoes, 6),
+            (echo_out, 6),
+            (products, 7),
+            (cubes, 4),
+            (distances, 7),
+            (similarity, 3),
+            (roots, 8),
+        ]
+        extra = {0: turn_exemplars, 2: quantize_exemplars, 3: setup_classes, 4: multiply_classes, 5: quantize_classes}
+
         with tc.manual_schedule():
             nc.vector.memset(tiny[:], 2.0**-100)
             nc.scalar.activation(out=warm[:], in_=tiny[:], func=ACT.Sqrt)
-            scale_row = f_scale.rearrange("o k -> (o k)")
-            for c in range(0, H, H // 2):
-                nc.scalar.dma_start(out=scale[:, c : c + H // 2], in_=scale_row[c : c + H // 2].partition_broadcast(P))
+            nc.vector.memset(scale_row[:], 0.0)
+            nc.scalar.dma_start(out=scale_row[0:1, :], in_=f_scale)
             load(0)
             ex_view = ex_n.rearrange("(m t) k -> m t k", t=4)
             for t in range(4):
                 nc.sync.dma_start(out=ex_raw[:, t, :], in_=ex_view[:, t, :])
+            load(1)
             nc.sync.dma_start(out=cls_raw[:], in_=ex_classes.rearrange("(m t) c -> m t c", t=4))
             nc.sync.dma_start(out=reps[:], in_=class_reps)
+            nc.gpsimd.memset(ones_f[:], 1.0)
             make_identity(nc, id_f[:])
             make_identity(nc, id_b[:])
             nc.gpsimd.memset(ones_b[:], 1.0)
-            nc.gpsimd.memset(ones_f[:], 1.0)
             nc.gpsimd.memset(norms[:], 0.0)
-            for pair in range(1, 8):
+            for pair in range(2, LEAD // 2):
                 load(pair)
-            chunks = [(blk, 0, 4) for blk in range(NBLK - 1)] + [(NBLK - 1, 0, 2), (NBLK - 1, 2, 2)]
-            last_pair = {2 * blk + (lo + n) // 2 - 1: (blk, lo, n) for blk, lo, n in chunks}
-            widen(0)
-            nc.scalar.copy(out=scale[:, H : 2 * H], in_=scale[:, 0:H])
-            setup_exemplars()
-            for i in range(PAIRS + 5):
-                if 8 + i < PAIRS:
-                    load(8 + i)
-                if i < PAIRS:
-                    if i > 0:
-                        widen(i)
-                    transposes(i)
-                    regroup(i)
-                if i == 1:
-                    setup_classes()
-                if i - 4 in last_pair:
-                    products(last_pair[i - 4])
-                if i - 3 in last_pair:
-                    quantize_a(last_pair[i - 3])
-                    echoes(last_pair[i - 3])
-                if 1 <= i <= PAIRS:
-                    quantize_x(i - 1)
-                    similarity(i - 1)
-                    squares(i - 1)
-                if 2 <= i <= PAIRS + 1:
-                    cubes(i - 2)
-                if i - 4 in last_pair:
-                    roots(last_pair[i - 4])
-                if i - 5 in last_pair:
-                    finish(last_pair[i - 5])
+            spread_scale()
+            for i in range(UNITS + 11):
+                if i % 2 == 0 and i + LEAD < UNITS:
+                    load((i + LEAD) // 2)
+                for step, lag in steps:
+                    if 0 <= i - lag < UNITS:
+                        step(i - lag)
+                if i in extra:
+                    extra[i]()

@@ -16,38 +16,40 @@ FP8 = mybir.dt.float8_e4m3fn
 FP8X4 = mybir.dt.float8_e4m3fn_x4
 ACT = mybir.ActivationFunctionType
 MULT = mybir.AluOpType.mult
+ADD = mybir.AluOpType.add
 SUB = mybir.AluOpType.subtract
 
 UNITS = B // P
-GROUP = 4
-LEAD = 10
+PAIRS = UNITS // 2
+SHARE = 320
+FIRST = 5
+LEAD = 4
 
 
 def tile_minerva_detex_pb_t_kernel(tc, f_bytes, f_scale, ex_n, ex_classes, class_reps, out):
     nc = tc.nc
     x_view = f_bytes.rearrange("(s p h j) k -> s h p (j k)", p=P, h=2, j=2)
-    out_view = out.rearrange("(s p j) k -> s p j k", p=P, j=GROUP)
+    out_view = out.rearrange("(s p j) k -> s p j k", p=P, j=4)
 
     with ExitStack() as ctx:
         keep = ctx.enter_context(tc.tile_pool(name="keep", bufs=1))
         xin = ctx.enter_context(tc.tile_pool(name="xin", bufs=16))
         work = ctx.enter_context(tc.tile_pool(name="work", bufs=4))
-        ps_x = ctx.enter_context(tc.psum_pool(name="ps_x", bufs=3))
-        ps_s = ctx.enter_context(tc.psum_pool(name="ps_s", bufs=2))
-        ps_e = ctx.enter_context(tc.psum_pool(name="ps_e", bufs=3))
+        ps_x = ctx.enter_context(tc.psum_pool(name="ps_x", bufs=2))
+        ps_s = ctx.enter_context(tc.psum_pool(name="ps_s", bufs=4))
+        ps_e = ctx.enter_context(tc.psum_pool(name="ps_e", bufs=2))
 
-        x_tiles, xs_tiles, xt_tiles, xg_tiles, xq_tiles = {}, {}, {}, {}, {}
+        x_tiles, raw_tiles, xs_tiles, xt_tiles, xg_tiles, xq_tiles = {}, {}, {}, {}, {}, {}
         s_tiles, sq_tiles, a_tiles, aq_tiles = {}, {}, {}, {}
-        ep_tiles, e_tiles, d2_tiles, root_tiles, res_tiles = {}, {}, {}, {}, {}
+        et_tiles, e_tiles, d_tiles, d2_tiles, root_tiles, back_tiles = {}, {}, {}, {}, {}, {}
 
         tiny = keep.tile([P, 1], F32)
         warm = keep.tile([P, 1], F32)
         id_f = keep.tile([P, P], F32)
         id_b = keep.tile([P, P], BF16)
-        ones_f = keep.tile([P, P], F32)
-        ones_b = keep.tile([P, P], BF16)
-        scale_row = keep.tile([P, H], F32)
-        scale = keep.tile([P, H], F32)
+        ones = keep.tile([P, P], F32)
+        scale_rows = keep.tile([P, P], F32)
+        scale = keep.tile([P, 2 * H], F32)
         ex_raw = keep.tile([P, 4, H], BF16, align_bytes=64)
         ex_grp = keep.tile([P, 4 * H], BF16, align_bytes=64)
         ex_codes = keep.tile([P, H], U32, align_bytes=64)
@@ -60,6 +62,7 @@ def tile_minerva_detex_pb_t_kernel(tc, f_bytes, f_scale, ex_n, ex_classes, class
         ec_scales = keep.tile([P, C], U8, align_bytes=64)
         reps_m2 = keep.tile([P, C], F32)
         reps_sq = keep.tile([P, C], F32)
+        ones_b = keep.tile([P, P], BF16)
         n_all = keep.tile([P, C], F32)
         n_hi = keep.tile([P, C], BF16)
         n_mid = keep.tile([P, C], BF16)
@@ -76,18 +79,25 @@ def tile_minerva_detex_pb_t_kernel(tc, f_bytes, f_scale, ex_n, ex_classes, class
                 nc.sync.dma_start(out=xb[:, c : c + step], in_=src[:, c : c + step])
             x_tiles[pair] = xb
 
-        def widen(u):
-            xs = work.tile([P, H], BF16, align_bytes=64)
-            c0 = (u % 2) * H
-            step = H // 2 if u == 0 else H
-            for c in range(0, H, step):
+        def widen(pair):
+            xs = work.tile([P, 2 * H], BF16, align_bytes=64)
+            cuts = [0, H // 4, H // 2, 3 * H // 4, H, 2 * H] if pair == 0 else [0, 2 * H]
+            if SHARE > 0 and FIRST <= pair < PAIRS - 1:
+                cuts = [0, 2 * H - SHARE + 16]
+            for c, e in zip(cuts[:-1], cuts[1:]):
                 nc.vector.tensor_tensor(
-                    out=xs[:, c : c + step],
-                    in0=x_tiles[u // 2][:, c0 + c : c0 + c + step].bitcast(FP8),
-                    in1=scale[:, c : c + step],
-                    op=MULT,
+                    out=xs[:, c:e], in0=x_tiles[pair][:, c:e].bitcast(FP8), in1=scale[:, c:e], op=MULT
                 )
-            xs_tiles[u] = xs
+            if SHARE > 0 and FIRST <= pair < PAIRS - 1:
+                part = slice(2 * H - SHARE, 2 * H)
+                nc.gpsimd.tensor_tensor(out=xs[:, part], in0=raw_tiles[pair][:], in1=scale[:, part], op=MULT)
+            xs_tiles[pair] = xs
+
+        def cast(pair):
+            if FIRST <= pair < PAIRS - 1:
+                raw = work.tile([P, SHARE], BF16)
+                nc.scalar.copy(out=raw[:], in_=x_tiles[pair][:, 2 * H - SHARE : 2 * H].bitcast(FP8))
+                raw_tiles[pair] = raw
 
         def turn(words, bank):
             for g in range(2):
@@ -102,27 +112,28 @@ def tile_minerva_detex_pb_t_kernel(tc, f_bytes, f_scale, ex_n, ex_classes, class
 
         def transposes(u):
             xt = ps_x.tile([P, 4, P], F32, tag="xt")
-            turn(xs_tiles[u][:].bitcast(F32), xt)
+            turn(xs_tiles[u // 2][:, (u % 2) * H : (u % 2 + 1) * H].bitcast(F32), xt)
             xt_tiles[u] = xt
 
         def regroup(u):
-            xg = work.tile([P, H], BF16, align_bytes=64)
-            leave(xg[:].bitcast(F32), xt_tiles[u])
-            xg_tiles[u] = xg
+            if u % 2 == 0:
+                xg = work.tile([P, 2 * H], BF16, align_bytes=64)
+                xg_tiles[u // 2] = xg
+            leave(xg_tiles[u // 2][:, (u % 2) * H : (u % 2 + 1) * H].bitcast(F32), xt_tiles[u])
 
-        def quantize_x(u):
-            xc = work.tile([P, 2 * P], U32, align_bytes=64)
-            xp = work.tile([P, 2 * P], U8, align_bytes=64)
-            nc.vector.quantize_mx(out=xc[:].bitcast(FP8X4), scales=xp[:], in_=xg_tiles[u][:])
-            xq_tiles[u] = (xc, xp)
+        def quantize_x(pair):
+            xc = work.tile([P, 4 * P], U32, align_bytes=64)
+            xp = work.tile([P, 4 * P], U8, align_bytes=64)
+            nc.vector.quantize_mx(out=xc[:].bitcast(FP8X4), scales=xp[:], in_=xg_tiles[pair][:])
+            xq_tiles[pair] = (xc, xp)
 
         def similarity(u):
-            xc, xp = xq_tiles[u]
+            xc, xp = xq_tiles[u // 2]
             s_ps = ps_s.tile([P, 4, P], F32, tag="s")
             for t in range(4):
                 for g in range(2):
                     w = slice((2 * t + g) * P, (2 * t + g + 1) * P)
-                    m = slice(g * P, (g + 1) * P)
+                    m = slice((2 * (u % 2) + g) * P, (2 * (u % 2) + g + 1) * P)
                     nc.tensor.matmul_mx(
                         out=s_ps[:, t, :],
                         lhsT=ex_codes[:, w].bitcast(FP8X4),
@@ -140,89 +151,138 @@ def tile_minerva_detex_pb_t_kernel(tc, f_bytes, f_scale, ex_n, ex_classes, class
             sq_tiles[u] = sq
 
         def cubes(u):
-            a_grp = work.tile([P, P, 4], BF16, align_bytes=64)
+            if u % 4 == 0:
+                a_grp = work.tile([P, 4 * P, 4], BF16, align_bytes=64)
+                a_tiles[u // 4] = a_grp
+            c0 = (u % 4) * P
             nc.vector.tensor_tensor(
-                out=a_grp[:], in0=s_tiles[u][:].rearrange("p t r -> p r t"), in1=sq_tiles[u][:], op=MULT
+                out=a_tiles[u // 4][:, c0 : c0 + P, :],
+                in0=s_tiles[u][:].rearrange("p t r -> p r t"),
+                in1=sq_tiles[u][:],
+                op=MULT,
             )
-            a_tiles[u] = a_grp
 
-        def quantize_a(u):
-            ac = work.tile([P, P], U32, align_bytes=64)
-            ap = work.tile([P, P], U8, align_bytes=64)
+        chunks = [(4 * b, 4) for b in range(UNITS // 4 - 1)] + [(UNITS - 4, 2), (UNITS - 2, 1), (UNITS - 1, 1)]
+
+        def quantize_a(chunk):
+            u, n = chunk
+            ac = work.tile([P, 4 * P], U32, align_bytes=64)
+            ap = work.tile([P, 4 * P], U8, align_bytes=64)
+            w = n * P
             nc.vector.quantize_mx(
-                out=ac[:].bitcast(FP8X4), scales=ap[:], in_=a_tiles[u][:].rearrange("p r t -> p (r t)")
+                out=ac[:, 0:w].bitcast(FP8X4),
+                scales=ap[:, 0:w],
+                in_=a_tiles[u // 4][:, (u % 4) * P : (u % 4) * P + w, :].rearrange("p r t -> p (r t)"),
             )
             aq_tiles[u] = (ac, ap)
 
-        def echoes(u):
+        def echoes(chunk):
+            u, n = chunk
             ac, ap = aq_tiles[u]
-            ep = ps_e.tile([P, 4, P], F32, tag="ep")
+            et_ps = ps_e.tile([P, 4 * P], F32, tag="ep")
             nc.tensor.matmul_mx(
-                out=ep[:, 0, :],
+                out=et_ps[:, 0 : n * P],
                 lhsT=ec_codes[:].bitcast(FP8X4),
                 lhsT_scale=ec_scales[:],
-                rhs=ac[:].bitcast(FP8X4),
-                rhs_scale=ap[:],
+                rhs=ac[:, 0 : n * P].bitcast(FP8X4),
+                rhs_scale=ap[:, 0 : n * P],
                 start=True,
                 stop=True,
             )
-            nc.tensor.matmul_mx(
-                out=ep[:, 1, :],
-                lhsT=ac[:].bitcast(FP8X4),
-                lhsT_scale=ap[:],
-                rhs=ec_codes[:].bitcast(FP8X4),
-                rhs_scale=ec_scales[:],
-                start=True,
-                stop=True,
-            )
-            ep_tiles[u] = ep
+            e_ps = ps_e.tile([P, 4, C], F32, tag="ep")
+            for j in range(n):
+                cols = slice(j * P, (j + 1) * P)
+                nc.tensor.matmul_mx(
+                    out=e_ps[:, j, :],
+                    lhsT=ac[:, cols].bitcast(FP8X4),
+                    lhsT_scale=ap[:, cols],
+                    rhs=ec_codes[:].bitcast(FP8X4),
+                    rhs_scale=ec_scales[:],
+                    start=True,
+                    stop=True,
+                )
+            et_tiles[u] = (et_ps, e_ps)
 
-        def echo_out(u):
-            ep = ep_tiles[u]
-            et = work.tile([P, P], F32)
-            nc.scalar.copy(out=et[:], in_=ep[:, 0, :])
-            junk = work.tile([P, C], F32)
-            e2 = work.tile([P, 1], F32)
-            nc.scalar.activation(out=junk[:], in_=ep[:, 1, :], func=ACT.Square, accum_out=e2[:])
+        def echo_out(chunk):
+            u, n = chunk
+            w = n * P
+            et_ps, e_ps = et_tiles[u]
+            et = work.tile([P, 4 * P], F32)
+            nc.scalar.copy(out=et[:, 0:w], in_=et_ps[:, 0:w])
+            junk = work.tile([P, 4, C], F32)
+            e2 = work.tile([P, 4], F32)
+            for j in range(n):
+                nc.scalar.activation(out=junk[:, j, :], in_=e_ps[:, j, :], func=ACT.Square, accum_out=e2[:, j : j + 1])
             e_tiles[u] = (et, e2)
 
-        def products(u):
+        def products(chunk):
+            u, n = chunk
             et, e2 = e_tiles[u]
-            d_ps = ep_tiles[u][:, 2, :]
-            nc.tensor.matmul(d_ps, ones_b[:], norms[:], start=True, stop=False)
-            nc.tensor.matmul(d_ps, et[:], reps_m2[:], start=False, stop=True)
+            d_ps = ps_e.tile([P, 4, C], F32, tag="ep")
+            for j in range(n):
+                nc.tensor.matmul(d_ps[:, j, :], ones_b[:], norms[:], start=True, stop=False)
+                nc.tensor.matmul(d_ps[:, j, :], et[:, j * P : (j + 1) * P], reps_m2[:], start=False, stop=True)
+            d_tiles[u] = d_ps
 
-        def distances(u):
-            et, e2 = e_tiles[u]
-            d2 = work.tile([P, C], F32)
-            nc.scalar.activation(out=d2[:], in_=ep_tiles[u][:, 2, :], func=ACT.Relu, bias=e2[:])
+        def distances(chunk):
+            u, n = chunk
+            e2 = e_tiles[u][1]
+            d2 = work.tile([P, 4, C], F32)
+            for j in range(n):
+                nc.scalar.activation(out=d2[:, j, :], in_=d_tiles[u][:, j, :], func=ACT.Relu, bias=e2[:, j : j + 1])
             d2_tiles[u] = d2
 
-        def roots(u):
-            root = work.tile([P, C], F32)
-            nc.scalar.activation(out=root[:], in_=d2_tiles[u][:], func=ACT.Sqrt, bias=tiny[:])
+        def roots(chunk):
+            u, n = chunk
+            root = work.tile([P, 4, C], F32)
+            nc.scalar.activation(out=root[:, 0:n, :], in_=d2_tiles[u][:, 0:n, :], func=ACT.Sqrt, bias=tiny[:])
             root_tiles[u] = root
 
-        def finish(u):
-            blk, j = u // GROUP, u % GROUP
-            if j == 0:
-                res = work.tile([P, GROUP, C], F32)
-                res_tiles[blk] = res
-            nc.scalar.mul(res_tiles[blk][:, j, :], root_tiles[u][:], -1.0)
-            width = 1 if blk == UNITS // GROUP - 1 else GROUP
-            if (j + 1) % width == 0:
-                js = slice(j + 1 - width, j + 1)
-                nc.sync.dma_start(out=out_view[blk, :, js, :], in_=res_tiles[blk][:, js, :])
+        def finish(chunk):
+            u, n = chunk
+            res = work.tile([P, 4, C], F32)
+            root = root_tiles[u]
+            if u < UNITS - 4:
+                nc.gpsimd.tensor_scalar(
+                    out=res[:, 0:n, :], in0=root[:, 0:n, :], scalar1=-1.0, scalar2=0.0, op0=MULT, op1=ADD
+                )
+            else:
+                nc.vector.tensor_scalar(
+                    out=res[:, 0:n, :], in0=root[:, 0:n, :], scalar1=-1.0, scalar2=None, op0=MULT
+                )
+            nc.sync.dma_start(out=out_view[u // 4, :, u % 4 : u % 4 + n, :], in_=res[:, 0:n, :])
+
+        def per_chunk(step):
+            def run(pair):
+                for chunk in chunks:
+                    if (chunk[0] + chunk[1] - 1) // 2 == pair:
+                        step(chunk)
+
+            return run
 
         def spread_scale():
+            warm_ps = ps_s.tile([P, P], F32, tag="s")
+            for c in range(4):
+                nc.tensor.matmul(warm_ps[:], ones[:], ones[:], start=True, stop=True)
             for c in range(2):
-                half = slice(c * H // 2, (c + 1) * H // 2)
                 s_ps = ps_s.tile([P, H // 2], F32, tag="s")
-                nc.tensor.matmul(s_ps[:], ones_f[:], scale_row[:, half], start=True, stop=True)
-                if c == 0:
-                    nc.vector.tensor_copy(out=scale[:, half], in_=s_ps[:])
-                else:
-                    nc.scalar.copy(out=scale[:, half], in_=s_ps[:])
+                for e in range(2):
+                    for j in range(2):
+                        row = 4 * c + 2 * e + j
+                        nc.tensor.matmul(
+                            s_ps[:, (2 * e + j) * P : (2 * e + j + 1) * P],
+                            id_f[:, row : row + 1].to_broadcast([P, P]),
+                            scale_rows[:],
+                            start=True,
+                            stop=True,
+                        )
+                    part = slice((2 * c + e) * H // 4, (2 * c + e + 1) * H // 4)
+                    bank = s_ps[:, e * H // 4 : (e + 1) * H // 4]
+                    if e == 0:
+                        nc.vector.tensor_copy(out=scale[:, part], in_=bank)
+                    else:
+                        nc.scalar.copy(out=scale[:, part], in_=bank)
+            nc.scalar.copy(out=scale[:, H : 2 * H], in_=scale[:, 0:H])
 
         def turn_exemplars():
             for t in range(4):
@@ -243,16 +303,16 @@ def tile_minerva_detex_pb_t_kernel(tc, f_bytes, f_scale, ex_n, ex_classes, class
                 nc.tensor.transpose(ct_ps[:, t, :], cls_raw[:, t, :], id_b[:])
             rt_ps = ps_e.tile([P, C], BF16, tag="ep")
             nc.tensor.transpose(rt_ps[:], reps[:], id_b[:])
+            nc.scalar.activation(out=reps_sq[:], in_=rt_ps[:], func=ACT.Square)
             nc.scalar.copy(out=cls_t[:], in_=ct_ps[:])
             nc.scalar.activation(out=reps_m2[:], in_=rt_ps[:], func=ACT.Copy, scale=-2.0)
-            nc.scalar.activation(out=reps_sq[:], in_=rt_ps[:], func=ACT.Square)
 
         def multiply_classes():
             ec_ps = ps_e.tile([P, 4, C], F32, tag="ep")
             for t in range(4):
                 nc.tensor.matmul(ec_ps[:, t, :], cls_t[:, t, :], reps[:], start=True, stop=True)
             n_ps = ps_e.tile([P, C], F32, tag="ep")
-            nc.tensor.matmul(n_ps[:], ones_f[:], reps_sq[:], start=True, stop=True)
+            nc.tensor.matmul(n_ps[:], ones[:], reps_sq[:], start=True, stop=True)
             nc.scalar.copy(out=ec_grp[:].rearrange("p (c t) -> p c t", t=4), in_=ec_ps[:].rearrange("p t c -> p c t"))
             nc.scalar.copy(out=n_all[:], in_=n_ps[:])
             nc.gpsimd.tensor_copy(out=n_hi[:], in_=n_all[:])
@@ -268,28 +328,34 @@ def tile_minerva_detex_pb_t_kernel(tc, f_bytes, f_scale, ex_n, ex_classes, class
             nc.vector.quantize_mx(out=ec_codes[:].bitcast(FP8X4), scales=ec_scales[:], in_=ec_grp[:])
 
         steps = [
-            (finish, 11),
+            (lambda pair: cubes(2 * pair + 0), 4),
+            (lambda pair: transposes(2 * pair + 0), 1),
+            (cast, 0),
+            (per_chunk(quantize_a), 5),
             (widen, 0),
+            (lambda pair: similarity(2 * pair + 0), 3),
             (quantize_x, 2),
-            (transposes, 1),
-            (squares, 4),
-            (regroup, 1),
-            (quantize_a, 5),
-            (echoes, 6),
-            (echo_out, 6),
-            (products, 7),
-            (cubes, 4),
-            (distances, 7),
-            (similarity, 3),
-            (roots, 8),
+            (lambda pair: similarity(2 * pair + 1), 3),
+            (lambda pair: transposes(2 * pair + 1), 1),
+            (per_chunk(roots), 8),
+            (per_chunk(echoes), 5),
+            (per_chunk(distances), 7),
+            (lambda pair: squares(2 * pair + 0), 3),
+            (per_chunk(finish), 10),
+            (lambda pair: regroup(2 * pair + 0), 1),
+            (lambda pair: squares(2 * pair + 1), 3),
+            (lambda pair: cubes(2 * pair + 1), 4),
+            (per_chunk(products), 6),
+            (per_chunk(echo_out), 5),
+            (lambda pair: regroup(2 * pair + 1), 1),
         ]
-        extra = {0: turn_exemplars, 2: quantize_exemplars, 3: setup_classes, 4: multiply_classes, 5: quantize_classes}
+        extra = {0: [turn_exemplars], 1: [quantize_exemplars, setup_classes], 2: [multiply_classes], 3: [quantize_classes]}
 
         with tc.manual_schedule():
+            nc.vector.memset(scale_rows[:], 0.0)
             nc.vector.memset(tiny[:], 2.0**-100)
             nc.scalar.activation(out=warm[:], in_=tiny[:], func=ACT.Sqrt)
-            nc.vector.memset(scale_row[:], 0.0)
-            nc.scalar.dma_start(out=scale_row[0:1, :], in_=f_scale)
+            nc.sync.dma_start(out=scale_rows[0 : H // P, :], in_=f_scale.rearrange("o (a b) -> (o a) b", b=P))
             load(0)
             ex_view = ex_n.rearrange("(m t) k -> m t k", t=4)
             for t in range(4):
@@ -297,19 +363,19 @@ def tile_minerva_detex_pb_t_kernel(tc, f_bytes, f_scale, ex_n, ex_classes, class
             load(1)
             nc.sync.dma_start(out=cls_raw[:], in_=ex_classes.rearrange("(m t) c -> m t c", t=4))
             nc.sync.dma_start(out=reps[:], in_=class_reps)
-            nc.gpsimd.memset(ones_f[:], 1.0)
+            nc.gpsimd.memset(ones[:], 1.0)
             make_identity(nc, id_f[:])
             make_identity(nc, id_b[:])
             nc.gpsimd.memset(ones_b[:], 1.0)
             nc.gpsimd.memset(norms[:], 0.0)
-            for pair in range(2, LEAD // 2):
+            for pair in range(2, LEAD):
                 load(pair)
             spread_scale()
-            for i in range(UNITS + 11):
-                if i % 2 == 0 and i + LEAD < UNITS:
-                    load((i + LEAD) // 2)
+            for i in range(PAIRS + 10):
+                if i + LEAD < PAIRS:
+                    load(i + LEAD)
                 for step, lag in steps:
-                    if 0 <= i - lag < UNITS:
+                    if 0 <= i - lag < PAIRS:
                         step(i - lag)
-                if i in extra:
-                    extra[i]()
+                for step in extra.get(i, []):
+                    step()

@@ -17,12 +17,11 @@ FP8X4 = mybir.dt.float8_e4m3fn_x4
 ACT = mybir.ActivationFunctionType
 MULT = mybir.AluOpType.mult
 ADD = mybir.AluOpType.add
+MAX = mybir.AluOpType.max
 SUB = mybir.AluOpType.subtract
 
 UNITS = B // P
 PAIRS = UNITS // 2
-SHARE = 320
-FIRST = 5
 LEAD = 4
 
 
@@ -35,11 +34,11 @@ def tile_minerva_detex_pb_t_kernel(tc, f_bytes, f_scale, ex_n, ex_classes, class
         keep = ctx.enter_context(tc.tile_pool(name="keep", bufs=1))
         xin = ctx.enter_context(tc.tile_pool(name="xin", bufs=16))
         work = ctx.enter_context(tc.tile_pool(name="work", bufs=4))
-        ps_x = ctx.enter_context(tc.psum_pool(name="ps_x", bufs=2))
-        ps_s = ctx.enter_context(tc.psum_pool(name="ps_s", bufs=4))
+        ps_x = ctx.enter_context(tc.psum_pool(name="ps_x", bufs=3))
+        ps_s = ctx.enter_context(tc.psum_pool(name="ps_s", bufs=3))
         ps_e = ctx.enter_context(tc.psum_pool(name="ps_e", bufs=2))
 
-        x_tiles, raw_tiles, xs_tiles, xt_tiles, xg_tiles, xq_tiles = {}, {}, {}, {}, {}, {}
+        x_tiles, xs_tiles, xt_tiles, xg_tiles, xq_tiles = {}, {}, {}, {}, {}
         s_tiles, sq_tiles, a_tiles, aq_tiles = {}, {}, {}, {}
         et_tiles, e_tiles, d_tiles, d2_tiles, root_tiles, back_tiles = {}, {}, {}, {}, {}, {}
 
@@ -82,22 +81,11 @@ def tile_minerva_detex_pb_t_kernel(tc, f_bytes, f_scale, ex_n, ex_classes, class
         def widen(pair):
             xs = work.tile([P, 2 * H], BF16, align_bytes=64)
             cuts = [0, H // 4, H // 2, 3 * H // 4, H, 2 * H] if pair == 0 else [0, 2 * H]
-            if SHARE > 0 and FIRST <= pair < PAIRS - 1:
-                cuts = [0, 2 * H - SHARE + 16]
             for c, e in zip(cuts[:-1], cuts[1:]):
                 nc.vector.tensor_tensor(
                     out=xs[:, c:e], in0=x_tiles[pair][:, c:e].bitcast(FP8), in1=scale[:, c:e], op=MULT
                 )
-            if SHARE > 0 and FIRST <= pair < PAIRS - 1:
-                part = slice(2 * H - SHARE, 2 * H)
-                nc.gpsimd.tensor_tensor(out=xs[:, part], in0=raw_tiles[pair][:], in1=scale[:, part], op=MULT)
             xs_tiles[pair] = xs
-
-        def cast(pair):
-            if FIRST <= pair < PAIRS - 1:
-                raw = work.tile([P, SHARE], BF16)
-                nc.scalar.copy(out=raw[:], in_=x_tiles[pair][:, 2 * H - SHARE : 2 * H].bitcast(FP8))
-                raw_tiles[pair] = raw
 
         def turn(words, bank):
             for g in range(2):
@@ -162,7 +150,7 @@ def tile_minerva_detex_pb_t_kernel(tc, f_bytes, f_scale, ex_n, ex_classes, class
                 op=MULT,
             )
 
-        chunks = [(4 * b, 4) for b in range(UNITS // 4 - 1)] + [(UNITS - 4, 2), (UNITS - 2, 1), (UNITS - 1, 1)]
+        chunks = [(4 * b, 4) for b in range(UNITS // 4 - 1)] + [(UNITS - 4, 2), (UNITS - 2, 2)]
 
         def quantize_a(chunk):
             u, n = chunk
@@ -176,10 +164,20 @@ def tile_minerva_detex_pb_t_kernel(tc, f_bytes, f_scale, ex_n, ex_classes, class
             )
             aq_tiles[u] = (ac, ap)
 
+        def late(u):
+            return u >= UNITS - 4
+
+        def bank(u):
+            if late(u):
+                ep = ps_s.tile([P, 4 * P], F32, tag="s")
+            else:
+                ep = ps_e.tile([P, 4 * P], F32, tag="ep")
+            return ep
+
         def echoes(chunk):
             u, n = chunk
             ac, ap = aq_tiles[u]
-            et_ps = ps_e.tile([P, 4 * P], F32, tag="ep")
+            et_ps = bank(u)
             nc.tensor.matmul_mx(
                 out=et_ps[:, 0 : n * P],
                 lhsT=ec_codes[:].bitcast(FP8X4),
@@ -189,11 +187,11 @@ def tile_minerva_detex_pb_t_kernel(tc, f_bytes, f_scale, ex_n, ex_classes, class
                 start=True,
                 stop=True,
             )
-            e_ps = ps_e.tile([P, 4, C], F32, tag="ep")
+            e_ps = bank(u)
             for j in range(n):
                 cols = slice(j * P, (j + 1) * P)
                 nc.tensor.matmul_mx(
-                    out=e_ps[:, j, :],
+                    out=e_ps[:, cols],
                     lhsT=ac[:, cols].bitcast(FP8X4),
                     lhsT_scale=ap[:, cols],
                     rhs=ec_codes[:].bitcast(FP8X4),
@@ -208,20 +206,24 @@ def tile_minerva_detex_pb_t_kernel(tc, f_bytes, f_scale, ex_n, ex_classes, class
             w = n * P
             et_ps, e_ps = et_tiles[u]
             et = work.tile([P, 4 * P], F32)
-            nc.scalar.copy(out=et[:, 0:w], in_=et_ps[:, 0:w])
+            if late(u):
+                nc.vector.tensor_copy(out=et[:, 0:w], in_=et_ps[:, 0:w])
+            else:
+                nc.scalar.copy(out=et[:, 0:w], in_=et_ps[:, 0:w])
             junk = work.tile([P, 4, C], F32)
             e2 = work.tile([P, 4], F32)
             for j in range(n):
-                nc.scalar.activation(out=junk[:, j, :], in_=e_ps[:, j, :], func=ACT.Square, accum_out=e2[:, j : j + 1])
+                nc.scalar.activation(out=junk[:, j, :], in_=e_ps[:, j * C : (j + 1) * C], func=ACT.Square, accum_out=e2[:, j : j + 1])
             e_tiles[u] = (et, e2)
 
         def products(chunk):
             u, n = chunk
             et, e2 = e_tiles[u]
-            d_ps = ps_e.tile([P, 4, C], F32, tag="ep")
+            d_ps = bank(u)
             for j in range(n):
-                nc.tensor.matmul(d_ps[:, j, :], ones_b[:], norms[:], start=True, stop=False)
-                nc.tensor.matmul(d_ps[:, j, :], et[:, j * P : (j + 1) * P], reps_m2[:], start=False, stop=True)
+                cols = slice(j * C, (j + 1) * C)
+                nc.tensor.matmul(d_ps[:, cols], ones_b[:], norms[:], start=True, stop=False)
+                nc.tensor.matmul(d_ps[:, cols], et[:, j * P : (j + 1) * P], reps_m2[:], start=False, stop=True)
             d_tiles[u] = d_ps
 
         def distances(chunk):
@@ -229,7 +231,13 @@ def tile_minerva_detex_pb_t_kernel(tc, f_bytes, f_scale, ex_n, ex_classes, class
             e2 = e_tiles[u][1]
             d2 = work.tile([P, 4, C], F32)
             for j in range(n):
-                nc.scalar.activation(out=d2[:, j, :], in_=d_tiles[u][:, j, :], func=ACT.Relu, bias=e2[:, j : j + 1])
+                d_in = d_tiles[u][:, j * C : (j + 1) * C]
+                if late(u) and 1:
+                    nc.vector.tensor_scalar(
+                        out=d2[:, j, :], in0=d_in, scalar1=e2[:, j : j + 1], scalar2=0.0, op0=ADD, op1=MAX
+                    )
+                else:
+                    nc.scalar.activation(out=d2[:, j, :], in_=d_in, func=ACT.Relu, bias=e2[:, j : j + 1])
             d2_tiles[u] = d2
 
         def roots(chunk):
@@ -242,14 +250,12 @@ def tile_minerva_detex_pb_t_kernel(tc, f_bytes, f_scale, ex_n, ex_classes, class
             u, n = chunk
             res = work.tile([P, 4, C], F32)
             root = root_tiles[u]
-            if u < UNITS - 4:
-                nc.gpsimd.tensor_scalar(
-                    out=res[:, 0:n, :], in0=root[:, 0:n, :], scalar1=-1.0, scalar2=0.0, op0=MULT, op1=ADD
-                )
-            else:
+            if late(u):
                 nc.vector.tensor_scalar(
                     out=res[:, 0:n, :], in0=root[:, 0:n, :], scalar1=-1.0, scalar2=None, op0=MULT
                 )
+            else:
+                nc.scalar.mul(res[:, 0:n, :], root[:, 0:n, :], -1.0)
             nc.sync.dma_start(out=out_view[u // 4, :, u % 4 : u % 4 + n, :], in_=res[:, 0:n, :])
 
         def per_chunk(step):
@@ -328,25 +334,24 @@ def tile_minerva_detex_pb_t_kernel(tc, f_bytes, f_scale, ex_n, ex_classes, class
             nc.vector.quantize_mx(out=ec_codes[:].bitcast(FP8X4), scales=ec_scales[:], in_=ec_grp[:])
 
         steps = [
-            (lambda pair: cubes(2 * pair + 0), 4),
-            (lambda pair: transposes(2 * pair + 0), 1),
-            (cast, 0),
-            (per_chunk(quantize_a), 5),
-            (widen, 0),
             (lambda pair: similarity(2 * pair + 0), 3),
-            (quantize_x, 2),
-            (lambda pair: similarity(2 * pair + 1), 3),
-            (lambda pair: transposes(2 * pair + 1), 1),
+            (lambda pair: transposes(2 * pair + 0), 1),
+            (lambda pair: cubes(2 * pair + 0), 4),
             (per_chunk(roots), 8),
+            (per_chunk(quantize_a), 5),
+            (per_chunk(finish), 9),
             (per_chunk(echoes), 5),
+            (lambda pair: similarity(2 * pair + 1), 3),
+            (lambda pair: cubes(2 * pair + 1), 4),
+            (lambda pair: transposes(2 * pair + 1), 1),
             (per_chunk(distances), 7),
             (lambda pair: squares(2 * pair + 0), 3),
-            (per_chunk(finish), 10),
             (lambda pair: regroup(2 * pair + 0), 1),
-            (lambda pair: squares(2 * pair + 1), 3),
-            (lambda pair: cubes(2 * pair + 1), 4),
-            (per_chunk(products), 6),
+            (quantize_x, 2),
             (per_chunk(echo_out), 5),
+            (widen, 0),
+            (lambda pair: squares(2 * pair + 1), 3),
+            (per_chunk(products), 6),
             (lambda pair: regroup(2 * pair + 1), 1),
         ]
         extra = {0: [turn_exemplars], 1: [quantize_exemplars, setup_classes], 2: [multiply_classes], 3: [quantize_classes]}
@@ -371,7 +376,7 @@ def tile_minerva_detex_pb_t_kernel(tc, f_bytes, f_scale, ex_n, ex_classes, class
             for pair in range(2, LEAD):
                 load(pair)
             spread_scale()
-            for i in range(PAIRS + 10):
+            for i in range(PAIRS + 9):
                 if i + LEAD < PAIRS:
                     load(i + LEAD)
                 for step, lag in steps:

from contextlib import ExitStack

import concourse.mybir as mybir
from concourse.masks import make_identity

B, D, H, C = 8192, 512, 1024, 128
P = 128

FLOPS = 2 * B * D * H + 2 * D * C * C + 2 * B * D * C + 3 * B * C * C

F32 = mybir.dt.float32
BF16 = mybir.dt.bfloat16
U32 = mybir.dt.uint32
U8 = mybir.dt.uint8
FP8 = mybir.dt.float8_e4m3fn
FP8X4 = mybir.dt.float8_e4m3fn_x4
ACT = mybir.ActivationFunctionType
MULT = mybir.AluOpType.mult
ADD = mybir.AluOpType.add
MAX = mybir.AluOpType.max
SUB = mybir.AluOpType.subtract

UNITS = B // P
PAIRS = UNITS // 2
LEAD = 4


def tile_minerva_detex_pb_t_kernel(tc, f_bytes, f_scale, ex_n, ex_classes, class_reps, out):
    nc = tc.nc
    x_view = f_bytes.rearrange("(s p h j) k -> s h p (j k)", p=P, h=2, j=2)
    out_view = out.rearrange("(s p j) k -> s p j k", p=P, j=4)

    with ExitStack() as ctx:
        keep = ctx.enter_context(tc.tile_pool(name="keep", bufs=1))
        xin = ctx.enter_context(tc.tile_pool(name="xin", bufs=16))
        work = ctx.enter_context(tc.tile_pool(name="work", bufs=4))
        ps_x = ctx.enter_context(tc.psum_pool(name="ps_x", bufs=3))
        ps_s = ctx.enter_context(tc.psum_pool(name="ps_s", bufs=3))
        ps_e = ctx.enter_context(tc.psum_pool(name="ps_e", bufs=2))

        x_tiles, xs_tiles, xt_tiles, xg_tiles, xq_tiles = {}, {}, {}, {}, {}
        s_tiles, sq_tiles, a_tiles, aq_tiles = {}, {}, {}, {}
        et_tiles, e_tiles, d_tiles, d2_tiles, root_tiles, back_tiles = {}, {}, {}, {}, {}, {}

        tiny = keep.tile([P, 1], F32)
        warm = keep.tile([P, 1], F32)
        id_f = keep.tile([P, P], F32)
        id_b = keep.tile([P, P], BF16)
        ones = keep.tile([P, P], F32)
        scale_rows = keep.tile([P, P], F32)
        scale = keep.tile([P, 2 * H], F32)
        ex_raw = keep.tile([P, 4, H], BF16, align_bytes=64)
        ex_grp = keep.tile([P, 4 * H], BF16, align_bytes=64)
        ex_codes = keep.tile([P, H], U32, align_bytes=64)
        ex_scales = keep.tile([P, H], U8, align_bytes=64)
        cls_raw = keep.tile([P, 4, C], BF16)
        cls_t = keep.tile([P, 4, P], BF16)
        reps = keep.tile([P, C], BF16)
        ec_grp = keep.tile([P, 4 * C], BF16, align_bytes=64)
        ec_codes = keep.tile([P, C], U32, align_bytes=64)
        ec_scales = keep.tile([P, C], U8, align_bytes=64)
        reps_m2 = keep.tile([P, C], F32)
        reps_sq = keep.tile([P, C], F32)
        ones_b = keep.tile([P, P], BF16)
        n_all = keep.tile([P, C], F32)
        n_hi = keep.tile([P, C], BF16)
        n_mid = keep.tile([P, C], BF16)
        n_lo = keep.tile([P, C], BF16)
        n_d1 = keep.tile([P, C], F32)
        n_d2 = keep.tile([P, C], F32)
        norms = keep.tile([P, C], BF16)

        def load(pair):
            xb = xin.tile([P, 2 * H], U8)
            src = x_view[pair // 2, pair % 2]
            step = H if pair == 0 else 2 * H
            for c in range(0, 2 * H, step):
                nc.sync.dma_start(out=xb[:, c : c + step], in_=src[:, c : c + step])
            x_tiles[pair] = xb

        def widen(pair):
            xs = work.tile([P, 2 * H], BF16, align_bytes=64)
            cuts = [0, H // 4, H // 2, 3 * H // 4, H, 2 * H] if pair == 0 else [0, 2 * H]
            for c, e in zip(cuts[:-1], cuts[1:]):
                nc.vector.tensor_tensor(
                    out=xs[:, c:e], in0=x_tiles[pair][:, c:e].bitcast(FP8), in1=scale[:, c:e], op=MULT
                )
            xs_tiles[pair] = xs

        def turn(words, bank):
            for g in range(2):
                for h in range(2):
                    nc.tensor.transpose(bank[:, 2 * g + h, :], words[:, 256 * g + h : 256 * (g + 1) : 2], id_f[:])

        def leave(grouped_words, bank):
            nc.scalar.copy(
                out=grouped_words.rearrange("p (g r h) -> p g r h", g=2, h=2),
                in_=bank[:].rearrange("p (g h) r -> p g r h", g=2),
            )

        def transposes(u):
            xt = ps_x.tile([P, 4, P], F32, tag="xt")
            turn(xs_tiles[u // 2][:, (u % 2) * H : (u % 2 + 1) * H].bitcast(F32), xt)
            xt_tiles[u] = xt

        def regroup(u):
            if u % 2 == 0:
                xg = work.tile([P, 2 * H], BF16, align_bytes=64)
                xg_tiles[u // 2] = xg
            leave(xg_tiles[u // 2][:, (u % 2) * H : (u % 2 + 1) * H].bitcast(F32), xt_tiles[u])

        def quantize_x(pair):
            xc = work.tile([P, 4 * P], U32, align_bytes=64)
            xp = work.tile([P, 4 * P], U8, align_bytes=64)
            nc.vector.quantize_mx(out=xc[:].bitcast(FP8X4), scales=xp[:], in_=xg_tiles[pair][:])
            xq_tiles[pair] = (xc, xp)

        def similarity(u):
            xc, xp = xq_tiles[u // 2]
            s_ps = ps_s.tile([P, 4, P], F32, tag="s")
            for t in range(4):
                for g in range(2):
                    w = slice((2 * t + g) * P, (2 * t + g + 1) * P)
                    m = slice((2 * (u % 2) + g) * P, (2 * (u % 2) + g + 1) * P)
                    nc.tensor.matmul_mx(
                        out=s_ps[:, t, :],
                        lhsT=ex_codes[:, w].bitcast(FP8X4),
                        lhsT_scale=ex_scales[:, w],
                        rhs=xc[:, m].bitcast(FP8X4),
                        rhs_scale=xp[:, m],
                        start=(g == 0),
                        stop=(g == 1),
                    )
            s_tiles[u] = s_ps

        def squares(u):
            sq = work.tile([P, P, 4], F32)
            nc.scalar.activation(out=sq[:], in_=s_tiles[u][:].rearrange("p t r -> p r t"), func=ACT.Square)
            sq_tiles[u] = sq

        def cubes(u):
            if u % 4 == 0:
                a_grp = work.tile([P, 4 * P, 4], BF16, align_bytes=64)
                a_tiles[u // 4] = a_grp
            c0 = (u % 4) * P
            nc.vector.tensor_tensor(
                out=a_tiles[u // 4][:, c0 : c0 + P, :],
                in0=s_tiles[u][:].rearrange("p t r -> p r t"),
                in1=sq_tiles[u][:],
                op=MULT,
            )

        chunks = [(4 * b, 4) for b in range(UNITS // 4 - 1)] + [(UNITS - 4, 2), (UNITS - 2, 2)]

        def quantize_a(chunk):
            u, n = chunk
            ac = work.tile([P, 4 * P], U32, align_bytes=64)
            ap = work.tile([P, 4 * P], U8, align_bytes=64)
            w = n * P
            nc.vector.quantize_mx(
                out=ac[:, 0:w].bitcast(FP8X4),
                scales=ap[:, 0:w],
                in_=a_tiles[u // 4][:, (u % 4) * P : (u % 4) * P + w, :].rearrange("p r t -> p (r t)"),
            )
            aq_tiles[u] = (ac, ap)

        def late(u):
            return u >= UNITS - 4

        def bank(u):
            if late(u):
                ep = ps_s.tile([P, 4 * P], F32, tag="s")
            else:
                ep = ps_e.tile([P, 4 * P], F32, tag="ep")
            return ep

        def echoes(chunk):
            u, n = chunk
            ac, ap = aq_tiles[u]
            et_ps = bank(u)
            nc.tensor.matmul_mx(
                out=et_ps[:, 0 : n * P],
                lhsT=ec_codes[:].bitcast(FP8X4),
                lhsT_scale=ec_scales[:],
                rhs=ac[:, 0 : n * P].bitcast(FP8X4),
                rhs_scale=ap[:, 0 : n * P],
                start=True,
                stop=True,
            )
            e_ps = bank(u)
            for j in range(n):
                cols = slice(j * P, (j + 1) * P)
                nc.tensor.matmul_mx(
                    out=e_ps[:, cols],
                    lhsT=ac[:, cols].bitcast(FP8X4),
                    lhsT_scale=ap[:, cols],
                    rhs=ec_codes[:].bitcast(FP8X4),
                    rhs_scale=ec_scales[:],
                    start=True,
                    stop=True,
                )
            et_tiles[u] = (et_ps, e_ps)

        def echo_out(chunk):
            u, n = chunk
            w = n * P
            et_ps, e_ps = et_tiles[u]
            et = work.tile([P, 4 * P], F32)
            if late(u):
                nc.vector.tensor_copy(out=et[:, 0:w], in_=et_ps[:, 0:w])
            else:
                nc.scalar.copy(out=et[:, 0:w], in_=et_ps[:, 0:w])
            junk = work.tile([P, 4, C], F32)
            e2 = work.tile([P, 4], F32)
            for j in range(n):
                nc.scalar.activation(out=junk[:, j, :], in_=e_ps[:, j * C : (j + 1) * C], func=ACT.Square, accum_out=e2[:, j : j + 1])
            e_tiles[u] = (et, e2)

        def products(chunk):
            u, n = chunk
            et, e2 = e_tiles[u]
            d_ps = bank(u)
            for j in range(n):
                cols = slice(j * C, (j + 1) * C)
                nc.tensor.matmul(d_ps[:, cols], ones_b[:], norms[:], start=True, stop=False)
                nc.tensor.matmul(d_ps[:, cols], et[:, j * P : (j + 1) * P], reps_m2[:], start=False, stop=True)
            d_tiles[u] = d_ps

        def distances(chunk):
            u, n = chunk
            e2 = e_tiles[u][1]
            d2 = work.tile([P, 4, C], F32)
            for j in range(n):
                d_in = d_tiles[u][:, j * C : (j + 1) * C]
                if late(u) and 1:
                    nc.vector.tensor_scalar(
                        out=d2[:, j, :], in0=d_in, scalar1=e2[:, j : j + 1], scalar2=0.0, op0=ADD, op1=MAX
                    )
                else:
                    nc.scalar.activation(out=d2[:, j, :], in_=d_in, func=ACT.Relu, bias=e2[:, j : j + 1])
            d2_tiles[u] = d2

        def roots(chunk):
            u, n = chunk
            root = work.tile([P, 4, C], F32)
            nc.scalar.activation(out=root[:, 0:n, :], in_=d2_tiles[u][:, 0:n, :], func=ACT.Sqrt, bias=tiny[:])
            root_tiles[u] = root

        def finish(chunk):
            u, n = chunk
            res = work.tile([P, 4, C], F32)
            root = root_tiles[u]
            if late(u):
                nc.vector.tensor_scalar(
                    out=res[:, 0:n, :], in0=root[:, 0:n, :], scalar1=-1.0, scalar2=None, op0=MULT
                )
            else:
                nc.scalar.mul(res[:, 0:n, :], root[:, 0:n, :], -1.0)
            nc.sync.dma_start(out=out_view[u // 4, :, u % 4 : u % 4 + n, :], in_=res[:, 0:n, :])

        def per_chunk(step):
            def run(pair):
                for chunk in chunks:
                    if (chunk[0] + chunk[1] - 1) // 2 == pair:
                        step(chunk)

            return run

        def spread_scale():
            warm_ps = ps_s.tile([P, P], F32, tag="s")
            for c in range(4):
                nc.tensor.matmul(warm_ps[:], ones[:], ones[:], start=True, stop=True)
            for c in range(2):
                s_ps = ps_s.tile([P, H // 2], F32, tag="s")
                for e in range(2):
                    for j in range(2):
                        row = 4 * c + 2 * e + j
                        nc.tensor.matmul(
                            s_ps[:, (2 * e + j) * P : (2 * e + j + 1) * P],
                            id_f[:, row : row + 1].to_broadcast([P, P]),
                            scale_rows[:],
                            start=True,
                            stop=True,
                        )
                    part = slice((2 * c + e) * H // 4, (2 * c + e + 1) * H // 4)
                    bank = s_ps[:, e * H // 4 : (e + 1) * H // 4]
                    if e == 0:
                        nc.vector.tensor_copy(out=scale[:, part], in_=bank)
                    else:
                        nc.scalar.copy(out=scale[:, part], in_=bank)
            nc.scalar.copy(out=scale[:, H : 2 * H], in_=scale[:, 0:H])

        def turn_exemplars():
            for t in range(4):
                xt = ps_x.tile([P, 4, P], F32, tag="xt")
                turn(ex_raw[:, t, :].bitcast(F32), xt)
                leave(ex_grp[:, t * H : (t + 1) * H].bitcast(F32), xt)

        def quantize_exemplars():
            for c in range(2):
                w = slice(c * H // 2, (c + 1) * H // 2)
                nc.vector.quantize_mx(
                    out=ex_codes[:, w].bitcast(FP8X4), scales=ex_scales[:, w], in_=ex_grp[:, 2 * c * H : 2 * (c + 1) * H]
                )

        def setup_classes():
            ct_ps = ps_e.tile([P, 4, P], BF16, tag="ep")
            for t in range(4):
                nc.tensor.transpose(ct_ps[:, t, :], cls_raw[:, t, :], id_b[:])
            rt_ps = ps_e.tile([P, C], BF16, tag="ep")
            nc.tensor.transpose(rt_ps[:], reps[:], id_b[:])
            nc.scalar.activation(out=reps_sq[:], in_=rt_ps[:], func=ACT.Square)
            nc.scalar.copy(out=cls_t[:], in_=ct_ps[:])
            nc.scalar.activation(out=reps_m2[:], in_=rt_ps[:], func=ACT.Copy, scale=-2.0)

        def multiply_classes():
            ec_ps = ps_e.tile([P, 4, C], F32, tag="ep")
            for t in range(4):
                nc.tensor.matmul(ec_ps[:, t, :], cls_t[:, t, :], reps[:], start=True, stop=True)
            n_ps = ps_e.tile([P, C], F32, tag="ep")
            nc.tensor.matmul(n_ps[:], ones[:], reps_sq[:], start=True, stop=True)
            nc.scalar.copy(out=ec_grp[:].rearrange("p (c t) -> p c t", t=4), in_=ec_ps[:].rearrange("p t c -> p c t"))
            nc.scalar.copy(out=n_all[:], in_=n_ps[:])
            nc.gpsimd.tensor_copy(out=n_hi[:], in_=n_all[:])
            nc.gpsimd.tensor_tensor(out=n_d1[:], in0=n_all[:], in1=n_hi[:], op=SUB)
            nc.gpsimd.tensor_copy(out=n_mid[:], in_=n_d1[:])
            nc.gpsimd.tensor_tensor(out=n_d2[:], in0=n_d1[:], in1=n_mid[:], op=SUB)
            nc.gpsimd.tensor_copy(out=n_lo[:], in_=n_d2[:])
            nc.gpsimd.tensor_scalar(out=norms[0:32, :], in0=n_hi[0:32, :], scalar1=1.0 / 32, scalar2=None, op0=MULT)
            nc.gpsimd.tensor_scalar(out=norms[32:64, :], in0=n_mid[32:64, :], scalar1=1.0 / 32, scalar2=None, op0=MULT)
            nc.gpsimd.tensor_scalar(out=norms[64:96, :], in0=n_lo[64:96, :], scalar1=1.0 / 32, scalar2=None, op0=MULT)

        def quantize_classes():
            nc.vector.quantize_mx(out=ec_codes[:].bitcast(FP8X4), scales=ec_scales[:], in_=ec_grp[:])

        steps = [
            (lambda pair: similarity(2 * pair + 0), 3),
            (lambda pair: transposes(2 * pair + 0), 1),
            (lambda pair: cubes(2 * pair + 0), 4),
            (per_chunk(roots), 8),
            (per_chunk(quantize_a), 5),
            (per_chunk(finish), 9),
            (per_chunk(echoes), 5),
            (lambda pair: similarity(2 * pair + 1), 3),
            (lambda pair: cubes(2 * pair + 1), 4),
            (lambda pair: transposes(2 * pair + 1), 1),
            (per_chunk(distances), 7),
            (lambda pair: squares(2 * pair + 0), 3),
            (lambda pair: regroup(2 * pair + 0), 1),
            (quantize_x, 2),
            (per_chunk(echo_out), 5),
            (widen, 0),
            (lambda pair: squares(2 * pair + 1), 3),
            (per_chunk(products), 6),
            (lambda pair: regroup(2 * pair + 1), 1),
        ]
        extra = {0: [turn_exemplars], 1: [quantize_exemplars, setup_classes], 2: [multiply_classes], 3: [quantize_classes]}

        with tc.manual_schedule():
            nc.vector.memset(scale_rows[:], 0.0)
            nc.vector.memset(tiny[:], 2.0**-100)
            nc.scalar.activation(out=warm[:], in_=tiny[:], func=ACT.Sqrt)
            nc.sync.dma_start(out=scale_rows[0 : H // P, :], in_=f_scale.rearrange("o (a b) -> (o a) b", b=P))
            load(0)
            ex_view = ex_n.rearrange("(m t) k -> m t k", t=4)
            for t in range(4):
                nc.sync.dma_start(out=ex_raw[:, t, :], in_=ex_view[:, t, :])
            load(1)
            nc.sync.dma_start(out=cls_raw[:], in_=ex_classes.rearrange("(m t) c -> m t c", t=4))
            nc.sync.dma_start(out=reps[:], in_=class_reps)
            nc.gpsimd.memset(ones[:], 1.0)
            make_identity(nc, id_f[:])
            make_identity(nc, id_b[:])
            nc.gpsimd.memset(ones_b[:], 1.0)
            nc.gpsimd.memset(norms[:], 0.0)
            for pair in range(2, LEAD):
                load(pair)
            spread_scale()
            for i in range(PAIRS + 9):
                if i + LEAD < PAIRS:
                    load(i + LEAD)
                for step, lag in steps:
                    if 0 <= i - lag < PAIRS:
                        step(i - lag)
                for step in extra.get(i, []):
                    step()
